import numpy as np
import ml_dtypes

BF16 = ml_dtypes.bfloat16


def bf(x):
    return np.asarray(x, np.float32).astype(BF16)


def f32(x):
    return np.asarray(x, np.float32)


def f64(x):
    return np.asarray(x).astype(np.float64)


def striped(idx):
    return np.tile(idx.reshape(-1, 16).T, (8, 1))


C, N, F, S = 128, 128, 128, 256


def sigmoid(v):
    return 1.0 / (1.0 + np.exp(-v))


def setup_inputs():
    return {
        "base": f32(np.random.standard_normal((C, S))),
        "x": bf(np.random.standard_normal((F, N))),
        "wa": bf(np.random.standard_normal((F, F)) / np.sqrt(F)),
        "wb": bf(np.random.standard_normal((F, F)) / np.sqrt(F)),
        "b1": f32(-3.0 + 0.5 * np.random.standard_normal((F, 1))),
        "adj": f32(np.random.uniform(0.0, 1.0, (C, N)) / 8.0),
        "offs": striped(np.random.permutation(S)[:N]),
    }


def reference(base, x, wa, wb, b1, adj, offs):
    idx = offs[:16].T.reshape(-1)
    a = f64(wa).T @ f64(x)
    b = f64(wb).T @ f64(x) + f64(b1)
    t = sigmoid(b.T[:, None, :] + a.T[None, :, :]).sum(axis=2)
    out = f64(base).copy()
    out[:, idx] = t * f64(adj)
    return out

@@ -1,0 +1,107 @@
+import concourse.mybir as mybir
+
+F32 = mybir.dt.float32
+BF16 = mybir.dt.bfloat16
+U16 = mybir.dt.uint16
+SIGMOID = mybir.ActivationFunctionType.Sigmoid
+ADD = mybir.AluOpType.add
+MULT = mybir.AluOpType.mult
+
+P = 128
+S = 256
+DIRECT = 4
+GROUPS = [4, 4, 4, 8, 8, 16, 16] + [16, 16, 16, 8, 4, 2, 1, 1]
+assert DIRECT + sum(GROUPS) == P
+H = 64
+
+FLOPS = 2 * (2 * P * P * P) + 2 * P * P * P
+
+
+def tile_graphconvolution_gi_kernel(tc, base, x, wa, wb, b1, adj, offs, out):
+    nc = tc.nc
+    with (
+        tc.tile_pool(name="held", bufs=1) as held,
+        tc.tile_pool(name="sums", bufs=6) as sums,
+        tc.tile_pool(name="gates", bufs=6) as gates,
+        tc.psum_pool(name="psum", bufs=1) as psum,
+    ):
+        x_sb = held.tile([P, P], BF16, name="x_sb")
+        wa_sb = held.tile([P, P], BF16, name="wa_sb")
+        wb_sb = held.tile([P, P], BF16, name="wb_sb")
+        b1_sb = held.tile([P, 1], F32, name="b1_sb")
+        adj_sb = held.tile([P, P], F32, name="adj_sb")
+        offsets = held.tile([P, P // 16], U16, name="offsets")
+        window = held.tile([P, S], F32, name="window")
+
+        nc.sync.dma_start(x_sb[:], x)
+        nc.scalar.dma_start(wb_sb[:], wb)
+        nc.sync.dma_start(wa_sb[:], wa)
+        nc.scalar.dma_start(b1_sb[:], b1)
+        nc.sync.dma_start(offsets[:], offs)
+        nc.sync.dma_start(adj_sb[:], adj)
+        nc.sync.dma_start(window[:], base)
+
+        ones = held.tile([P, 1], BF16, name="ones")
+        nc.vector.memset(ones[:], 1.0)
+        warm = held.tile([P, 1], BF16, name="warm")
+        nc.scalar.activation(warm[:], ones[:], SIGMOID)
+
+        early = DIRECT + GROUPS[0]
+        b_ps = psum.tile([P, P], F32, name="b_ps")
+        a_early_ps = psum.tile([P, early], F32, name="a_early_ps")
+        a_late_ps = psum.tile([P, P - early], F32, name="a_late_ps")
+        nc.tensor.matmul(b_ps[:], wb_sb[:], x_sb[:], start=True, stop=True)
+        nc.tensor.matmul(a_early_ps[:], wa_sb[:], x_sb[:, 0:early], start=True, stop=True)
+        nc.tensor.matmul(a_late_ps[:], wa_sb[:], x_sb[:, early:P], start=True, stop=True)
+        ab1_sb = held.tile([P, P], F32, name="ab1_sb")
+        b_sb = held.tile([P, P], F32, name="b_sb")
+        nc.vector.tensor_copy(b_sb[:], b_ps[:])
+        nc.vector.tensor_scalar(ab1_sb[:, 0:early], a_early_ps[:], b1_sb[:, 0:1], None, ADD)
+
+        t_ps = [psum.tile([P, H], F32, name=f"t_ps{half}") for half in range(P // H)]
+        t_sb = [held.tile([P, H], F32, name=f"t_sb{half}") for half in range(P // H)]
+
+        def sum_over_features(gate, first, nodes):
+            for i in range(nodes):
+                j = first + i
+                nc.tensor.matmul(
+                    t_ps[j // H][:, j % H : j % H + 1],
+                    gate[:, i * P : (i + 1) * P],
+                    ones[:],
+                    start=True,
+                    stop=True,
+                )
+
+        gate = gates.tile([P, DIRECT * P], BF16, name="gate")
+        for j in range(DIRECT):
+            nc.scalar.activation(
+                gate[:, j * P : (j + 1) * P], b_sb[:], SIGMOID, bias=ab1_sb[:, j : j + 1]
+            )
+        sum_over_features(gate, 0, DIRECT)
+
+        first = DIRECT
+        for nodes in GROUPS:
+            pair_sum = sums.tile([P, nodes * P], F32, name="pair_sum")
+            for i in range(nodes):
+                j = first + i
+                nc.vector.tensor_scalar(
+                    pair_sum[:, i * P : (i + 1) * P], b_sb[:], ab1_sb[:, j : j + 1], None, ADD
+                )
+            if first == DIRECT:
+                nc.vector.tensor_scalar(
+                    ab1_sb[:, early:P], a_late_ps[:], b1_sb[:, 0:1], None, ADD
+                )
+            gate = gates.tile([P, nodes * P], BF16, name="gate")
+            nc.scalar.activation(gate[:], pair_sum[:], SIGMOID)
+            sum_over_features(gate, first, nodes)
+            first += nodes
+            if first % H == 0:
+                half = first // H - 1
+                nc.vector.tensor_copy(t_sb[half][:], t_ps[half][:])
+                nc.vector.tensor_tensor(
+                    window[:].indirect(offsets[:, half * (H // 16) : (half + 1) * (H // 16)]),
+                    t_sb[half][:],
+                    adj_sb[:, half * H : (half + 1) * H],
+                    MULT,
+                )
+        nc.sync.dma_start(out, window[:])

@@ -10,7 +10,7 @@ MULT = mybir.AluOpType.mult
 P = 128
 S = 256
 DIRECT = 4
-GROUPS = [4, 4, 4, 8, 8, 16, 16] + [16, 16, 16, 8, 4, 2, 1, 1]
+GROUPS = [4, 6, 8, 12, 18, 24, 24, 16, 8, 2, 1, 1]
 assert DIRECT + sum(GROUPS) == P
 H = 64
 
@@ -80,6 +80,7 @@ def tile_graphconvolution_gi_kernel(tc, base, x, wa, wb, b1, adj, offs, out):
         sum_over_features(gate, 0, DIRECT)
 
         first = DIRECT
+        placed = 0
         for nodes in GROUPS:
             pair_sum = sums.tile([P, nodes * P], F32, name="pair_sum")
             for i in range(nodes):
@@ -95,8 +96,9 @@ def tile_graphconvolution_gi_kernel(tc, base, x, wa, wb, b1, adj, offs, out):
             nc.scalar.activation(gate[:], pair_sum[:], SIGMOID)
             sum_over_features(gate, first, nodes)
             first += nodes
-            if first % H == 0:
-                half = first // H - 1
+            if first // H > placed:
+                half = placed
+                placed += 1
                 nc.vector.tensor_copy(t_sb[half][:], t_ps[half][:])
                 nc.vector.tensor_tensor(
                     window[:].indirect(offsets[:, half * (H // 16) : (half + 1) * (H // 16)]),

@@ -10,7 +10,8 @@ MULT = mybir.AluOpType.mult
 P = 128
 S = 256
 DIRECT = 4
-GROUPS = [4, 6, 8, 12, 18, 24, 24, 16, 8, 2, 1, 1]
+GROUPS = [4, 6, 9, 13, 19, 28] + [28, 12, 4, 1]
+LAST = 5
 assert DIRECT + sum(GROUPS) == P
 H = 64
 
@@ -59,13 +60,18 @@ def tile_graphconvolution_gi_kernel(tc, base, x, wa, wb, b1, adj, offs, out):
         nc.vector.tensor_scalar(ab1_sb[:, 0:early], a_early_ps[:], b1_sb[:, 0:1], None, ADD)
 
         t_ps = [psum.tile([P, H], F32, name=f"t_ps{half}") for half in range(P // H)]
+        t_last_ps = psum.tile([P, LAST], F32, name="t_last_ps")
         t_sb = [held.tile([P, H], F32, name=f"t_sb{half}") for half in range(P // H)]
 
         def sum_over_features(gate, first, nodes):
             for i in range(nodes):
                 j = first + i
+                if j < P - LAST:
+                    t_column = t_ps[j // H][:, j % H : j % H + 1]
+                else:
+                    t_column = t_last_ps[:, j - (P - LAST) : j - (P - LAST) + 1]
                 nc.tensor.matmul(
-                    t_ps[j // H][:, j % H : j % H + 1],
+                    t_column,
                     gate[:, i * P : (i + 1) * P],
                     ones[:],
                     start=True,
@@ -96,10 +102,15 @@ def tile_graphconvolution_gi_kernel(tc, base, x, wa, wb, b1, adj, offs, out):
             nc.scalar.activation(gate[:], pair_sum[:], SIGMOID)
             sum_over_features(gate, first, nodes)
             first += nodes
+            if first == P - LAST:
+                nc.vector.tensor_copy(t_sb[1][:, 0 : H - LAST], t_ps[1][:, 0 : H - LAST])
             if first // H > placed:
                 half = placed
                 placed += 1
-                nc.vector.tensor_copy(t_sb[half][:], t_ps[half][:])
+                if first < P:
+                    nc.vector.tensor_copy(t_sb[half][:], t_ps[half][:])
+                else:
+                    nc.vector.tensor_copy(t_sb[half][:, H - LAST : H], t_last_ps[:])
                 nc.vector.tensor_tensor(
                     window[:].indirect(offsets[:, half * (H // 16) : (half + 1) * (H // 16)]),
                     t_sb[half][:],

@@ -1,4 +1,5 @@
 import concourse.mybir as mybir
+from concourse.masks import make_identity
 
 F32 = mybir.dt.float32
 BF16 = mybir.dt.bfloat16
@@ -10,9 +11,10 @@ MULT = mybir.AluOpType.mult
 P = 128
 S = 256
 DIRECT = 4
-GROUPS = [4, 6, 9, 13, 19, 28] + [28, 12, 4, 1]
+GROUPS = [4, 6, 9, 13, 19, 28] + [28, 10, 3, 2]
+TURNED = 2
 LAST = 5
-assert DIRECT + sum(GROUPS) == P
+assert DIRECT + sum(GROUPS) + TURNED == P
 H = 64
 
 FLOPS = 2 * (2 * P * P * P) + 2 * P * P * P
@@ -44,6 +46,10 @@ def tile_graphconvolution_gi_kernel(tc, base, x, wa, wb, b1, adj, offs, out):
 
         ones = held.tile([P, 1], BF16, name="ones")
         nc.vector.memset(ones[:], 1.0)
+        ones_square = held.tile([P, P], F32, name="ones_square")
+        nc.gpsimd.memset(ones_square[:], 1.0)
+        identity = held.tile([P, P], F32, name="identity")
+        make_identity(nc, identity[:])
         warm = held.tile([P, 1], BF16, name="warm")
         nc.scalar.activation(warm[:], ones[:], SIGMOID)
 
@@ -59,17 +65,21 @@ def tile_graphconvolution_gi_kernel(tc, base, x, wa, wb, b1, adj, offs, out):
         nc.vector.tensor_copy(b_sb[:], b_ps[:])
         nc.vector.tensor_scalar(ab1_sb[:, 0:early], a_early_ps[:], b1_sb[:, 0:1], None, ADD)
 
-        t_ps = [psum.tile([P, H], F32, name=f"t_ps{half}") for half in range(P // H)]
+        t_ps = [
+            psum.tile([P, TURNED * P], F32, name="t_ps0", tag="bank_in_turn"),
+            psum.tile([P, H], F32, name="t_ps1"),
+        ]
         t_last_ps = psum.tile([P, LAST], F32, name="t_last_ps")
         t_sb = [held.tile([P, H], F32, name=f"t_sb{half}") for half in range(P // H)]
 
         def sum_over_features(gate, first, nodes):
             for i in range(nodes):
                 j = first + i
-                if j < P - LAST:
+                if j < P - TURNED - LAST:
                     t_column = t_ps[j // H][:, j % H : j % H + 1]
                 else:
-                    t_column = t_last_ps[:, j - (P - LAST) : j - (P - LAST) + 1]
+                    k = j - (P - TURNED - LAST)
+                    t_column = t_last_ps[:, k : k + 1]
                 nc.tensor.matmul(
                     t_column,
                     gate[:, i * P : (i + 1) * P],
@@ -77,6 +87,14 @@ def tile_graphconvolution_gi_kernel(tc, base, x, wa, wb, b1, adj, offs, out):
                     start=True,
                     stop=True,
                 )
+
+        def place(half):
+            nc.vector.tensor_tensor(
+                window[:].indirect(offsets[:, half * (H // 16) : (half + 1) * (H // 16)]),
+                t_sb[half][:],
+                adj_sb[:, half * H : (half + 1) * H],
+                MULT,
+            )
 
         gate = gates.tile([P, DIRECT * P], BF16, name="gate")
         for j in range(DIRECT):
@@ -86,7 +104,6 @@ def tile_graphconvolution_gi_kernel(tc, base, x, wa, wb, b1, adj, offs, out):
         sum_over_features(gate, 0, DIRECT)
 
         first = DIRECT
-        placed = 0
         for nodes in GROUPS:
             pair_sum = sums.tile([P, nodes * P], F32, name="pair_sum")
             for i in range(nodes):
@@ -102,19 +119,42 @@ def tile_graphconvolution_gi_kernel(tc, base, x, wa, wb, b1, adj, offs, out):
             nc.scalar.activation(gate[:], pair_sum[:], SIGMOID)
             sum_over_features(gate, first, nodes)
             first += nodes
-            if first == P - LAST:
-                nc.vector.tensor_copy(t_sb[1][:, 0 : H - LAST], t_ps[1][:, 0 : H - LAST])
-            if first // H > placed:
-                half = placed
-                placed += 1
-                if first < P:
-                    nc.vector.tensor_copy(t_sb[half][:], t_ps[half][:])
-                else:
-                    nc.vector.tensor_copy(t_sb[half][:, H - LAST : H], t_last_ps[:])
-                nc.vector.tensor_tensor(
-                    window[:].indirect(offsets[:, half * (H // 16) : (half + 1) * (H // 16)]),
-                    t_sb[half][:],
-                    adj_sb[:, half * H : (half + 1) * H],
-                    MULT,
+            if first - nodes < H <= first:
+                nc.vector.tensor_copy(t_sb[0][:], t_ps[0][:, 0:H])
+                place(0)
+                diagonals = sums.tile([P, TURNED * P], F32, name="pair_sum")
+                turned_ps = psum.tile(
+                    [P, TURNED * P], F32, name="turned_ps", tag="bank_in_turn"
                 )
+                for i in range(TURNED):
+                    j = P - TURNED + i
+                    block = slice(i * P, (i + 1) * P)
+                    nc.vector.tensor_scalar(
+                        diagonals[:, block], identity[:], ab1_sb[:, j : j + 1], None, MULT
+                    )
+                    nc.tensor.matmul(
+                        turned_ps[:, block], x_sb[:], wb_sb[:], start=True, stop=False
+                    )
+                    nc.tensor.matmul(
+                        turned_ps[:, block],
+                        ones_square[:],
+                        diagonals[:, block],
+                        start=False,
+                        stop=True,
+                    )
+            if first == P - TURNED - LAST:
+                nc.vector.tensor_copy(
+                    t_sb[1][:, 0 : H - TURNED - LAST], t_ps[1][:, 0 : H - TURNED - LAST]
+                )
+        nc.vector.tensor_copy(t_sb[1][:, H - TURNED - LAST : H - TURNED], t_last_ps[:])
+        for i in range(TURNED):
+            gate = gates.tile([P, P], BF16, name="gate")
+            column = H - TURNED + i
+            nc.scalar.activation(
+                gate[:],
+                turned_ps[:, i * P : (i + 1) * P],
+                SIGMOID,
+                accum_out=t_sb[1][:, column : column + 1],
+            )
+        place(1)
         nc.sync.dma_start(out, window[:])

@@ -11,9 +11,9 @@ MULT = mybir.AluOpType.mult
 P = 128
 S = 256
 DIRECT = 4
-GROUPS = [4, 6, 9, 13, 19, 28] + [28, 10, 3, 2]
-TURNED = 2
-LAST = 5
+GROUPS = [4, 6, 9, 13, 19, 28] + [28, 10, 4]
+TURNED = 3
+LAST = 4
 assert DIRECT + sum(GROUPS) + TURNED == P
 H = 64
 

import concourse.mybir as mybir
from concourse.masks import make_identity

F32 = mybir.dt.float32
BF16 = mybir.dt.bfloat16
U16 = mybir.dt.uint16
SIGMOID = mybir.ActivationFunctionType.Sigmoid
ADD = mybir.AluOpType.add
MULT = mybir.AluOpType.mult

P = 128
S = 256
DIRECT = 4
GROUPS = [4, 6, 9, 13, 19, 28] + [28, 10, 4]
TURNED = 3
LAST = 4
assert DIRECT + sum(GROUPS) + TURNED == P
H = 64

FLOPS = 2 * (2 * P * P * P) + 2 * P * P * P


def tile_graphconvolution_gi_kernel(tc, base, x, wa, wb, b1, adj, offs, out):
    nc = tc.nc
    with (
        tc.tile_pool(name="held", bufs=1) as held,
        tc.tile_pool(name="sums", bufs=6) as sums,
        tc.tile_pool(name="gates", bufs=6) as gates,
        tc.psum_pool(name="psum", bufs=1) as psum,
    ):
        x_sb = held.tile([P, P], BF16, name="x_sb")
        wa_sb = held.tile([P, P], BF16, name="wa_sb")
        wb_sb = held.tile([P, P], BF16, name="wb_sb")
        b1_sb = held.tile([P, 1], F32, name="b1_sb")
        adj_sb = held.tile([P, P], F32, name="adj_sb")
        offsets = held.tile([P, P // 16], U16, name="offsets")
        window = held.tile([P, S], F32, name="window")

        nc.sync.dma_start(x_sb[:], x)
        nc.scalar.dma_start(wb_sb[:], wb)
        nc.sync.dma_start(wa_sb[:], wa)
        nc.scalar.dma_start(b1_sb[:], b1)
        nc.sync.dma_start(offsets[:], offs)
        nc.sync.dma_start(adj_sb[:], adj)
        nc.sync.dma_start(window[:], base)

        ones = held.tile([P, 1], BF16, name="ones")
        nc.vector.memset(ones[:], 1.0)
        ones_square = held.tile([P, P], F32, name="ones_square")
        nc.gpsimd.memset(ones_square[:], 1.0)
        identity = held.tile([P, P], F32, name="identity")
        make_identity(nc, identity[:])
        warm = held.tile([P, 1], BF16, name="warm")
        nc.scalar.activation(warm[:], ones[:], SIGMOID)

        early = DIRECT + GROUPS[0]
        b_ps = psum.tile([P, P], F32, name="b_ps")
        a_early_ps = psum.tile([P, early], F32, name="a_early_ps")
        a_late_ps = psum.tile([P, P - early], F32, name="a_late_ps")
        nc.tensor.matmul(b_ps[:], wb_sb[:], x_sb[:], start=True, stop=True)
        nc.tensor.matmul(a_early_ps[:], wa_sb[:], x_sb[:, 0:early], start=True, stop=True)
        nc.tensor.matmul(a_late_ps[:], wa_sb[:], x_sb[:, early:P], start=True, stop=True)
        ab1_sb = held.tile([P, P], F32, name="ab1_sb")
        b_sb = held.tile([P, P], F32, name="b_sb")
        nc.vector.tensor_copy(b_sb[:], b_ps[:])
        nc.vector.tensor_scalar(ab1_sb[:, 0:early], a_early_ps[:], b1_sb[:, 0:1], None, ADD)

        t_ps = [
            psum.tile([P, TURNED * P], F32, name="t_ps0", tag="bank_in_turn"),
            psum.tile([P, H], F32, name="t_ps1"),
        ]
        t_last_ps = psum.tile([P, LAST], F32, name="t_last_ps")
        t_sb = [held.tile([P, H], F32, name=f"t_sb{half}") for half in range(P // H)]

        def sum_over_features(gate, first, nodes):
            for i in range(nodes):
                j = first + i
                if j < P - TURNED - LAST:
                    t_column = t_ps[j // H][:, j % H : j % H + 1]
                else:
                    k = j - (P - TURNED - LAST)
                    t_column = t_last_ps[:, k : k + 1]
                nc.tensor.matmul(
                    t_column,
                    gate[:, i * P : (i + 1) * P],
                    ones[:],
                    start=True,
                    stop=True,
                )

        def place(half):
            nc.vector.tensor_tensor(
                window[:].indirect(offsets[:, half * (H // 16) : (half + 1) * (H // 16)]),
                t_sb[half][:],
                adj_sb[:, half * H : (half + 1) * H],
                MULT,
            )

        gate = gates.tile([P, DIRECT * P], BF16, name="gate")
        for j in range(DIRECT):
            nc.scalar.activation(
                gate[:, j * P : (j + 1) * P], b_sb[:], SIGMOID, bias=ab1_sb[:, j : j + 1]
            )
        sum_over_features(gate, 0, DIRECT)

        first = DIRECT
        for nodes in GROUPS:
            pair_sum = sums.tile([P, nodes * P], F32, name="pair_sum")
            for i in range(nodes):
                j = first + i
                nc.vector.tensor_scalar(
                    pair_sum[:, i * P : (i + 1) * P], b_sb[:], ab1_sb[:, j : j + 1], None, ADD
                )
            if first == DIRECT:
                nc.vector.tensor_scalar(
                    ab1_sb[:, early:P], a_late_ps[:], b1_sb[:, 0:1], None, ADD
                )
            gate = gates.tile([P, nodes * P], BF16, name="gate")
            nc.scalar.activation(gate[:], pair_sum[:], SIGMOID)
            sum_over_features(gate, first, nodes)
            first += nodes
            if first - nodes < H <= first:
                nc.vector.tensor_copy(t_sb[0][:], t_ps[0][:, 0:H])
                place(0)
                diagonals = sums.tile([P, TURNED * P], F32, name="pair_sum")
                turned_ps = psum.tile(
                    [P, TURNED * P], F32, name="turned_ps", tag="bank_in_turn"
                )
                for i in range(TURNED):
                    j = P - TURNED + i
                    block = slice(i * P, (i + 1) * P)
                    nc.vector.tensor_scalar(
                        diagonals[:, block], identity[:], ab1_sb[:, j : j + 1], None, MULT
                    )
                    nc.tensor.matmul(
                        turned_ps[:, block], x_sb[:], wb_sb[:], start=True, stop=False
                    )
                    nc.tensor.matmul(
                        turned_ps[:, block],
                        ones_square[:],
                        diagonals[:, block],
                        start=False,
                        stop=True,
                    )
            if first == P - TURNED - LAST:
                nc.vector.tensor_copy(
                    t_sb[1][:, 0 : H - TURNED - LAST], t_ps[1][:, 0 : H - TURNED - LAST]
                )
        nc.vector.tensor_copy(t_sb[1][:, H - TURNED - LAST : H - TURNED], t_last_ps[:])
        for i in range(TURNED):
            gate = gates.tile([P, P], BF16, name="gate")
            column = H - TURNED + i
            nc.scalar.activation(
                gate[:],
                turned_ps[:, i * P : (i + 1) * P],
                SIGMOID,
                accum_out=t_sb[1][:, column : column + 1],
            )
        place(1)
        nc.sync.dma_start(out, window[:])
